import numpy as np
import ml_dtypes


def mxq(x, axis, fmt="e4m3"):
    dtype, down = {"e4m3": (ml_dtypes.float8_e4m3fn, 7), "e5m2": (ml_dtypes.float8_e5m2, 14)}[fmt]
    v = np.moveaxis(np.asarray(x, np.float32).astype(ml_dtypes.bfloat16).astype(np.float64), axis, -1)
    blocks = v.reshape(v.shape[:-1] + (-1, 32))
    amax = np.abs(blocks).max(-1, keepdims=True)
    byte = np.maximum(np.where(amax > 0, np.frexp(amax)[1] - 1 + 127, 0) - down, 1)
    scale = np.exp2(byte - 127.0)
    codes = (blocks / scale).astype(np.float32).astype(dtype).astype(np.float64)
    return np.moveaxis((codes * scale).reshape(v.shape), -1, axis)


WIDE = False


def mx_kscale(k):
    if not WIDE:
        return np.ones(k)
    levels = np.array([10, -10, 5, -5, 0])
    if k % 512:
        return np.exp2(np.random.permutation(np.resize(levels, k // 32))).repeat(32)
    a = np.empty((k // 512, 16))
    for p in range(k // 512):
        a[p, :8] = np.random.permutation(np.resize(levels, 8))
        for g in range(8):
            far = levels[np.abs(levels - a[p, g]) >= 10]
            a[p, g + 8] = far[np.random.randint(len(far))]
    return np.exp2(a.ravel()).repeat(32)


BF16 = ml_dtypes.bfloat16


def bf(x):
    return np.asarray(x, np.float32).astype(BF16)


def f64(x):
    return np.asarray(x).astype(np.float64)


B, D, E, NM = 512, 1024, 1024, 4


def draw0():
    s, t = mx_kscale(D), mx_kscale(D)
    gain = np.ones((E, NM))
    gain[:, 1] = 0.3
    off = np.zeros((E, NM))
    off[:, 1] = 1.3 * np.sign(np.random.standard_normal(E))
    return {
        "prev_act": bf(np.maximum(np.random.standard_normal((B, D)) * 1.2, 0.0) * s),
        "W1": bf(np.random.standard_normal((D, D)) / np.sqrt(D) / s[:, None] * t),
        "b1": bf(np.random.standard_normal(D) * 0.2 * t),
        "W2": bf(np.random.standard_normal((D, NM * E)) / np.sqrt(D) * gain.reshape(-1) / t[:, None]),
        "b2": bf(np.random.standard_normal(NM * E) * 0.1 + off.reshape(-1)),
        "dopamine": bf(np.random.standard_normal((B, E))),
        "serotonin": bf(np.random.standard_normal((B, E))),
        "glutamate": bf(np.random.standard_normal((B, E))),
        "gaba": bf(np.random.standard_normal((B, E))),
    }


def core(prev_act, W1, b1, W2, b2, dopamine, serotonin, glutamate, gaba):
    hid = np.maximum((mxq(f64(prev_act), 1, "e4m3") @ mxq(f64(W1), 0, "e4m3")) + f64(b1), 0.0)
    h = np.tanh((mxq(hid, 1, "e4m3") @ mxq(f64(W2), 0, "e4m3")) + f64(b2))
    preds = h.reshape(B, E, NM)
    p_dop, p_ser, p_glu, p_gab = preds[..., 0], preds[..., 1], preds[..., 2], preds[..., 3]
    inv = 1.0 / np.maximum(np.abs(p_ser), 1e-6)
    dop = f64(dopamine) + p_dop * inv
    ser = f64(serotonin) + p_ser
    glu = f64(glutamate) + p_glu * inv
    gab = f64(gaba) + p_gab * inv
    return np.concatenate([dop, ser, glu, gab], axis=0)


def e4m3fn_bytes(y):
    return np.clip(np.asarray(y, np.float64), -448.0, 448.0).astype(np.float32).astype(ml_dtypes.float8_e4m3fn).view(np.uint8)


def e4m3fn_values(b):
    return np.asarray(b, np.uint8).view(ml_dtypes.float8_e4m3fn).astype(np.float64)


def setup_inputs():
    d = draw0()
    x0 = np.asarray(d['W2']).astype(np.float64)
    s = (np.max(np.abs(x0), axis=(1,), keepdims=True) / 448.0).astype(np.float32)
    out = {}
    for k, v in d.items():
        if k == 'W2':
            out['W2_bytes'] = e4m3fn_bytes(x0 / s.astype(np.float64))
            out['W2_scale'] = s
        else:
            out[k] = v
    return out


def reference(prev_act, W1, b1, W2_bytes, W2_scale, b2, dopamine, serotonin, glutamate, gaba):
    return core(prev_act, W1, b1, e4m3fn_values(W2_bytes) * W2_scale.astype(np.float64), b2, dopamine, serotonin, glutamate, gaba)

@@ -1,0 +1,409 @@
+from contextlib import ExitStack
+
+import concourse.mybir as mybir
+from concourse.masks import make_identity
+
+F32 = mybir.dt.float32
+BF16 = mybir.dt.bfloat16
+U32 = mybir.dt.uint32
+U8 = mybir.dt.uint8
+FP8 = mybir.dt.float8_e4m3fn
+FP8X4 = mybir.dt.float8_e4m3fn_x4
+ACT = mybir.ActivationFunctionType
+ALU = mybir.AluOpType
+
+P = 128
+B, D, E, NM = 512, 1024, 1024, 4
+G = 2
+BB = 4
+JB = 8
+CW = 1024
+HC = 8
+DOP, SER, GLU, GAB = 0, 1, 2, 3
+
+FLOPS = 2 * B * D * D + 2 * B * D * NM * E
+
+JP = JB // 2
+WIDEN_ON_VECTOR = (4, 0, 0, 0, 0, 0, 0, 1, 1, 1, 1, 1, 1, 2, 2, 2)
+DUE = (2, 2, 3, 3, 3, 3, 3, 3, 3)
+SERDUE = (0, 0, 0, 0, 0, 1, 1, 1, 1)
+EVAC_ON_VECTOR = tuple((jb, SER) for jb in range(8)) + tuple((jb, DOP) for jb in range(6)) + ((6, GAB), (7, GAB))
+
+
+def tile_hebbianlayer_pb_kernel(
+    tc, prev_act, W1, b1, W2_bytes, W2_scale, b2, dopamine, serotonin, glutamate, gaba, out
+):
+    nc = tc.nc
+    with ExitStack() as ctx:
+        keep = ctx.enter_context(tc.tile_pool(name="keep", bufs=1))
+        stage = ctx.enter_context(tc.tile_pool(name="stage", bufs=3))
+        psum = ctx.enter_context(tc.psum_pool(name="psum", bufs=4))
+        ctx.enter_context(tc.manual_schedule())
+
+        ident = keep.tile([P, P], F32, name="ident")
+        make_identity(nc, ident[:])
+        ident_bf = keep.tile([P, P], BF16, name="ident_bf")
+        nc.vector.tensor_copy(out=ident_bf[:], in_=ident[:])
+
+        w2s = keep.tile([P, G, 4], F32, name="w2s")
+        nc.scalar.dma_start(out=w2s[:], in_=W2_scale.rearrange("(g p t) o -> p g (t o)", g=G, p=P, t=4))
+        b1_raw = keep.tile([P, G, 4], BF16, name="b1_raw")
+        nc.scalar.dma_start(out=b1_raw[:], in_=b1.rearrange("(g p t) -> p g t", g=G, p=P, t=4))
+        b2_raw = keep.tile([P, JB, NM], BF16, name="b2_raw")
+        nc.scalar.dma_start(out=b2_raw[:], in_=b2.rearrange("(jb p c) -> p jb c", jb=JB, p=P, c=NM))
+
+        warm = keep.tile([P, 1], F32, name="warm")
+        nc.vector.memset(warm[:], 0.0)
+        nc.scalar.activation(out=warm[:], in_=warm[:], func=ACT.Tanh)
+
+        w2_v = W2_bytes.rearrange("(g p t) n -> g p t n", g=G, p=P, t=4)
+        w1_v = W1.rearrange("(g p t) n -> g p t n", g=G, p=P, t=4)
+        act_v = prev_act.rearrange("(bb p) k -> p bb k", p=P)
+        w2b = []
+
+        def load_w2():
+            hc = len(w2b)
+            ch, g = divmod(hc, 2)
+            t = stage.tile([P, 4, CW], U8, tag="w2bytes", name="w2bytes", bufs=5)
+            nc.sync.dma_start(out=t[:], in_=w2_v[g][:, :, ch * CW : (ch + 1) * CW])
+            w2b.append(t)
+
+        load_w2()
+        load_w2()
+        act_raw = stage.tile([P, BB, D], BF16, tag="big", name="act_raw", align_bytes=64, bufs=4)
+        for h in range(2):
+            nc.sync.dma_start(out=act_raw[:, 2 * h : 2 * h + 2, :], in_=act_v[:, 2 * h : 2 * h + 2, :])
+        w1_raw = []
+
+        def load_w1(g):
+            t = stage.tile([P, 4, D], BF16, tag="big", name="w1_raw", align_bytes=64, bufs=4)
+            nc.sync.dma_start(out=t[:], in_=w1_v[g])
+            w1_raw.append(t)
+
+        load_w1(0)
+        load_w1(1)
+        for i in range(3):
+            load_w2()
+        adds = {}
+
+        def load_add(c, src):
+            adds[c] = keep.tile([P, BB, E], BF16, name="add_%d" % c)
+            nc.sync.dma_start(out=adds[c][:], in_=src.rearrange("(bb p) j -> p bb j", p=P))
+
+        act_c = keep.tile([P, G, B], U32, name="act_c", align_bytes=64)
+        act_s = keep.tile([P, G, B], U8, name="act_s", align_bytes=64)
+        w1_c = keep.tile([P, G, D], U32, name="w1_c", align_bytes=64)
+        w1_s = keep.tile([P, G, D], U8, name="w1_s", align_bytes=64)
+        hid_c = keep.tile([P, G, B], U32, name="hid_c", align_bytes=64)
+        hid_s = keep.tile([P, G, B], U8, name="hid_s", align_bytes=64)
+        w2_c = keep.tile([P, G, NM * E], U32, name="w2_c", align_bytes=64)
+        w2_s = keep.tile([P, G, NM * E], U8, name="w2_s", align_bytes=64)
+
+        b1f = keep.tile([P, G, 4], F32, name="b1f")
+        b2f = keep.tile([P, JB, NM], F32, name="b2f")
+
+        wide = {}
+        inter = {}
+
+        def widen(jb, g, nv):
+            t = stage.tile([P, 4, 4 * P], BF16, tag="wide", name="w2_wide", align_bytes=64, bufs=4)
+            wide[jb, g] = t
+            half = 512 * (jb % 2)
+            for j in range(4):
+                src = w2b[2 * (jb // 2) + g][:, j, half : half + 512].bitcast(FP8)
+                if j < nv:
+                    nc.vector.tensor_scalar(
+                        out=t[:, j, :], in0=src, scalar1=w2s[:, g, j : j + 1], scalar2=None, op0=ALU.mult
+                    )
+                else:
+                    nc.scalar.activation(out=t[:, j, :], in_=src, func=ACT.Copy, scale=w2s[:, g, j : j + 1])
+
+        def interleave(jb, g):
+            inter[jb, g] = stage.tile([P, NM, P, 4], BF16, tag="inter", name="w2_i", align_bytes=64, bufs=3)
+            nc.vector.tensor_copy(
+                out=inter[jb, g][:].rearrange("p c m t -> p m t c"),
+                in_=wide[jb, g][:].rearrange("p t (m c) -> p m t c", c=NM),
+            )
+
+        def quantise(jb, g):
+            cols = slice(512 * jb, 512 * (jb + 1))
+            nc.vector.quantize_mx(
+                out=w2_c[:, g, cols].bitcast(FP8X4),
+                scales=w2_s[:, g, cols],
+                in_=inter[jb, g][:].rearrange("p c m t -> p (c m t)"),
+            )
+
+        words = act_raw[:].bitcast(F32)
+        act_i = stage.tile([P, G, B, 4], BF16, tag="big", name="act_i", align_bytes=64, bufs=4)
+        act_iw = act_i[:].rearrange("p g b t -> p g (b t)").bitcast(F32)
+
+        def act_turn(h):
+            for g in range(G):
+                bank = psum.tile([P, 2, 2, P], F32, tag="tr", name="act_t")
+                for i in range(2):
+                    for u in range(2):
+                        nc.tensor.transpose(
+                            bank[:, i, u, :], words[:, 2 * h + i, 256 * g + u : 256 * (g + 1) : 2], ident[:]
+                        )
+                dst = act_iw[:, g, 512 * h : 512 * (h + 1)].rearrange("p (i r u) -> p i r u", i=2, u=2)
+                src = bank[:].rearrange("p i u r -> p i r u")
+                if g == 0:
+                    nc.scalar.copy(out=dst, in_=src)
+                else:
+                    nc.vector.tensor_copy(out=dst, in_=src)
+
+        def act_quantise(g):
+            nc.vector.quantize_mx(
+                out=act_c[:, g, :].bitcast(FP8X4),
+                scales=act_s[:, g, :],
+                in_=act_i[:, g].rearrange("p b t -> p (b t)"),
+            )
+
+        w1_i = {}
+
+        def w1_interleave(g, h):
+            if h == 0:
+                w1_i[g] = stage.tile([P, 2, 4, P, 4], BF16, tag="big", name="w1_i", align_bytes=64, bufs=4)
+            nc.vector.tensor_copy(
+                out=w1_i[g][:, h].rearrange("p t m j -> p m j t"),
+                in_=w1_raw[g][:, :, 512 * h : 512 * (h + 1)].rearrange("p j (m t) -> p m j t", t=4),
+            )
+
+        def w1_quantise(g, h):
+            cols = slice(512 * h, 512 * (h + 1))
+            nc.vector.quantize_mx(
+                out=w1_c[:, g, cols].bitcast(FP8X4),
+                scales=w1_s[:, g, cols],
+                in_=w1_i[g][:, h].rearrange("p t m j -> p (t m j)"),
+            )
+
+        hid = {}
+
+        def hidden(h, on_vector=()):
+            if h == 0:
+                hid[0] = stage.tile([P, G, 4, B], BF16, tag="big", name="hid", align_bytes=64, bufs=4)
+            for t in range(4):
+                bank = psum.tile([P, B], F32, tag="mm", name="mm")
+                cols = slice(512 * h + P * t, 512 * h + P * (t + 1))
+                for g in range(G):
+                    nc.tensor.matmul_mx(
+                        out=bank[:],
+                        lhsT=w1_c[:, g, cols].bitcast(FP8X4),
+                        lhsT_scale=w1_s[:, g, cols],
+                        rhs=act_c[:, g, :].bitcast(FP8X4),
+                        rhs_scale=act_s[:, g, :],
+                        start=(g == 0),
+                        stop=(g == G - 1),
+                    )
+                if t in on_vector:
+                    nc.vector.tensor_scalar(
+                        out=hid[0][:, h, t, :], in0=bank[:], scalar1=b1f[:, h, t : t + 1], scalar2=0.0, op0=ALU.add, op1=ALU.max
+                    )
+                else:
+                    nc.scalar.activation(out=hid[0][:, h, t, :], in_=bank[:], func=ACT.Relu, bias=b1f[:, h, t : t + 1])
+
+        def hidden_interleave(h):
+            if h == 0:
+                hid[1] = stage.tile([P, G, B, 4], BF16, tag="big", name="hid_i", align_bytes=64, bufs=4)
+            nc.vector.tensor_copy(
+                out=hid[1][:, h].rearrange("p (n i) t -> p n t i", i=4),
+                in_=hid[0][:, h].rearrange("p t (n i) -> p n t i", i=4),
+            )
+
+        def hidden_quantise(h):
+            nc.vector.quantize_mx(
+                out=hid_c[:, h, :].bitcast(FP8X4),
+                scales=hid_s[:, h, :],
+                in_=hid[1][:, h].rearrange("p b t -> p (b t)"),
+            )
+
+        pred = keep.tile([P, JP, NM, 2, B], F32, name="pred")
+
+        def predict(jb, c):
+            bank = psum.tile([P, B], F32, tag="mm", name="mm")
+            cols = slice(512 * jb + P * c, 512 * jb + P * (c + 1))
+            for g in range(G):
+                nc.tensor.matmul_mx(
+                    out=bank[:],
+                    lhsT=w2_c[:, g, cols].bitcast(FP8X4),
+                    lhsT_scale=w2_s[:, g, cols],
+                    rhs=hid_c[:, g, :].bitcast(FP8X4),
+                    rhs_scale=hid_s[:, g, :],
+                    start=(g == 0),
+                    stop=(g == G - 1),
+                )
+            nc.scalar.activation(
+                out=pred[:, jb // 2, c, jb % 2, :], in_=bank[:], func=ACT.Tanh, bias=b2f[:, jb, c : c + 1]
+            )
+
+        outs = {}
+        out_v = out.rearrange("(c bb p) j -> c p bb j", c=NM, bb=BB)
+        banks = {}
+
+        def turn(jb, c, tag="tr"):
+            if tag == "tr":
+                bank = psum.tile([P, BB, P], F32, tag="tr", name="tr")
+            else:
+                bank = psum.tile([P, BB, P], F32, tag="mm", name="tr")
+            banks[jb, c] = bank
+            jcols = slice(P * jb, P * (jb + 1))
+            on_vector = (jb, c) in EVAC_ON_VECTOR
+            if not on_vector:
+                nc.tensor.matmul(bank[:], lhsT=ident_bf[:], rhs=adds[c][:, :, jcols], start=True, stop=False)
+            for bb in range(BB):
+                nc.tensor.matmul(
+                    bank[:, bb, :],
+                    lhsT=pred[:, jb // 2, c, jb % 2, P * bb : P * (bb + 1)],
+                    rhs=ident[:],
+                    start=on_vector,
+                    stop=on_vector or bb == BB - 1,
+                    is_transpose=True,
+                )
+
+        def finish(jb, c):
+            bank = banks.pop((jb, c))
+            jcols = slice(P * jb, P * (jb + 1))
+            part = slice(P * (jb % 2), P * (jb % 2 + 1))
+            if jb % 2 == 0:
+                if c == SER:
+                    ser_out = stage.tile([P, BB, 2 * P], F32, tag="wide", name="ser_out", bufs=4, align_bytes=64)
+                    outs[c] = ser_out[:]
+                else:
+                    outs[c] = pred[:, jb // 2, c].rearrange("p h b -> p (h b)").rearrange("p (bb j) -> p bb j", bb=BB)
+            dst = outs[c][:, :, part]
+            if (jb, c) in EVAC_ON_VECTOR:
+                nc.vector.tensor_tensor(out=dst, in0=bank[:], in1=adds[c][:, :, jcols], op=ALU.add)
+            else:
+                nc.scalar.copy(out=dst, in_=bank[:])
+            if jb % 2 == 1:
+                nc.sync.dma_start(out=out_v[c][:, :, P * (jb - 1) : P * (jb + 1)], in_=outs[c])
+
+        inv = {}
+
+        def invert(jp):
+            if jp % 2 == 0:
+                inv[jp // 2] = stage.tile([P, 2, 2, B], F32, tag="big", name="inv", align_bytes=64, bufs=4)
+            y = inv[jp // 2][:, jp % 2]
+            nc.scalar.activation(out=y, in_=pred[:, jp, SER], func=ACT.Abs_reciprocal_sqrt)
+
+        def square(jp, on_vector=False):
+            y = inv[jp // 2][:, jp % 2]
+            if on_vector:
+                nc.vector.tensor_tensor(out=y, in0=y, in1=y, op=ALU.mult)
+            else:
+                nc.scalar.activation(out=y, in_=y, func=ACT.Square)
+
+        def scale(jp, c):
+            nc.vector.scalar_tensor_tensor(
+                out=pred[:, jp, c],
+                in0=inv[jp // 2][:, jp % 2],
+                scalar=1e6,
+                in1=pred[:, jp, c],
+                op0=ALU.min,
+                op1=ALU.mult,
+            )
+
+        units = [(0, 0), (1, 0), (0, 1), (1, 1)] + [(jb, g) for jb in range(2, 8) for g in range(2)]
+
+        def W(i):
+            widen(units[i][0], units[i][1], WIDEN_ON_VECTOR[i])
+
+        def I(i):
+            interleave(*units[i])
+
+        def Q(i):
+            quantise(*units[i])
+
+        W(0)
+        W(1)
+        I(0)
+        W(2)
+        act_turn(0)
+        act_turn(1)
+        nc.vector.tensor_copy(out=b1f[:], in_=b1_raw[:])
+        nc.vector.tensor_copy(out=b2f[:], in_=b2_raw[:])
+        Q(0)
+        I(1)
+        act_quantise(0)
+        act_quantise(1)
+        Q(1)
+        W(3)
+        w1_interleave(0, 0)
+        w1_interleave(0, 1)
+        w1_quantise(0, 0)
+        w1_interleave(1, 0)
+        w1_quantise(0, 1)
+        w1_interleave(1, 1)
+        w1_quantise(1, 0)
+        I(2)
+        w1_quantise(1, 1)
+        W(4)
+        W(5)
+        I(3)
+        Q(2)
+        load_w2()
+        hidden(0)
+        hidden(1)
+        Q(3)
+        I(4)
+        W(6)
+        Q(4)
+        hidden_interleave(0)
+        I(5)
+        hidden_quantise(0)
+        hidden_interleave(1)
+        Q(5)
+        hidden_quantise(1)
+        load_w2()
+        W(7)
+        I(6)
+        load_w2()
+        load_add(SER, serotonin)
+        load_add(DOP, dopamine)
+        load_add(GLU, glutamate)
+        load_add(GAB, gaba)
+        order = [(jb, c) for jb in range(8) for c in (SER, DOP, GLU, GAB)]
+        done = 0
+        for i in range(7, 16):
+            if i + 1 < 16:
+                W(i + 1)
+            I(i)
+            Q(i - 1)
+            for k in range(DUE[i - 7]):
+                predict(*order.pop(0))
+            for k in range(SERDUE[i - 7]):
+                turn(done, SER)
+                if done > 0:
+                    finish(done - 1, SER)
+                done += 1
+        Q(15)
+        while order[0][0] < 7:
+            predict(*order.pop(0))
+        while done < 7:
+            turn(done, SER)
+            finish(done - 1, SER)
+            done += 1
+        predict(*order.pop(0))
+        turn(7, SER)
+        while order:
+            predict(*order.pop(0))
+        finish(6, SER)
+        finish(7, SER)
+        invert(0)
+        square(0)
+        invert(1)
+        square(1)
+        for jp in range(4):
+            for c in (DOP, GLU, GAB):
+                scale(jp, c)
+                if c == DOP and jp + 2 < 4:
+                    invert(jp + 2)
+                    square(jp + 2)
+                for jb in (2 * jp, 2 * jp + 1):
+                    turn(jb, c, "mm" if c == GLU else "tr")
+                if c == GLU:
+                    for jb in (2 * jp, 2 * jp + 1):
+                        finish(jb, DOP)
+            for c in (GLU, GAB):
+                for jb in (2 * jp, 2 * jp + 1):
+                    finish(jb, c)

@@ -24,10 +24,9 @@ DOP, SER, GLU, GAB = 0, 1, 2, 3
 FLOPS = 2 * B * D * D + 2 * B * D * NM * E
 
 JP = JB // 2
-WIDEN_ON_VECTOR = (4, 0, 0, 0, 0, 0, 0, 1, 1, 1, 1, 1, 1, 2, 2, 2)
-DUE = (2, 2, 3, 3, 3, 3, 3, 3, 3)
-SERDUE = (0, 0, 0, 0, 0, 1, 1, 1, 1)
-EVAC_ON_VECTOR = tuple((jb, SER) for jb in range(8)) + tuple((jb, DOP) for jb in range(6)) + ((6, GAB), (7, GAB))
+WIDEN_ON_VECTOR = (4, 0, 0, 0, 0, 0, 0, 1, 1, 2, 2, 2, 2, 2, 2, 2)
+DUE = (2, 2, 3, 3, 3, 3, 4, 4, 4)
+EVAC_ON_VECTOR = tuple((jb, SER) for jb in range(8)) + tuple((jb, GAB) for jb in (0, 2, 4, 6)) + ((6, GLU),)
 
 
 def tile_hebbianlayer_pb_kernel(
@@ -48,9 +47,7 @@ def tile_hebbianlayer_pb_kernel(
         w2s = keep.tile([P, G, 4], F32, name="w2s")
         nc.scalar.dma_start(out=w2s[:], in_=W2_scale.rearrange("(g p t) o -> p g (t o)", g=G, p=P, t=4))
         b1_raw = keep.tile([P, G, 4], BF16, name="b1_raw")
-        nc.scalar.dma_start(out=b1_raw[:], in_=b1.rearrange("(g p t) -> p g t", g=G, p=P, t=4))
         b2_raw = keep.tile([P, JB, NM], BF16, name="b2_raw")
-        nc.scalar.dma_start(out=b2_raw[:], in_=b2.rearrange("(jb p c) -> p jb c", jb=JB, p=P, c=NM))
 
         warm = keep.tile([P, 1], F32, name="warm")
         nc.vector.memset(warm[:], 0.0)
@@ -64,8 +61,13 @@ def tile_hebbianlayer_pb_kernel(
         def load_w2():
             hc = len(w2b)
             ch, g = divmod(hc, 2)
-            t = stage.tile([P, 4, CW], U8, tag="w2bytes", name="w2bytes", bufs=5)
-            nc.sync.dma_start(out=t[:], in_=w2_v[g][:, :, ch * CW : (ch + 1) * CW])
+            t = stage.tile([P, 4, CW], U8, tag="w2bytes", name="w2bytes", bufs=4)
+            if hc == 0:
+                for h in range(2):
+                    cols = slice(512 * h, 512 * (h + 1))
+                    nc.sync.dma_start(out=t[:, :, cols], in_=w2_v[g][:, :, cols])
+            else:
+                nc.sync.dma_start(out=t[:], in_=w2_v[g][:, :, ch * CW : (ch + 1) * CW])
             w2b.append(t)
 
         load_w2()
@@ -82,7 +84,9 @@ def tile_hebbianlayer_pb_kernel(
 
         load_w1(0)
         load_w1(1)
-        for i in range(3):
+        nc.sync.dma_start(out=b1_raw[:], in_=b1.rearrange("(g p t) -> p g t", g=G, p=P, t=4))
+        nc.sync.dma_start(out=b2_raw[:], in_=b2.rearrange("(jb p c) -> p jb c", jb=JB, p=P, c=NM))
+        for i in range(2):
             load_w2()
         adds = {}
 
@@ -106,7 +110,7 @@ def tile_hebbianlayer_pb_kernel(
         inter = {}
 
         def widen(jb, g, nv):
-            t = stage.tile([P, 4, 4 * P], BF16, tag="wide", name="w2_wide", align_bytes=64, bufs=4)
+            t = stage.tile([P, 4, 4 * P], BF16, tag="wide", name="w2_wide", align_bytes=64, bufs=5)
             wide[jb, g] = t
             half = 512 * (jb % 2)
             for j in range(4):
@@ -121,8 +125,8 @@ def tile_hebbianlayer_pb_kernel(
         def interleave(jb, g):
             inter[jb, g] = stage.tile([P, NM, P, 4], BF16, tag="inter", name="w2_i", align_bytes=64, bufs=3)
             nc.vector.tensor_copy(
-                out=inter[jb, g][:].rearrange("p c m t -> p m t c"),
-                in_=wide[jb, g][:].rearrange("p t (m c) -> p m t c", c=NM),
+                out=inter[jb, g][:].rearrange("p c m t -> p m c t"),
+                in_=wide[jb, g][:].rearrange("p t (m c) -> p m c t", c=NM),
             )
 
         def quantise(jb, g):
@@ -165,8 +169,8 @@ def tile_hebbianlayer_pb_kernel(
             if h == 0:
                 w1_i[g] = stage.tile([P, 2, 4, P, 4], BF16, tag="big", name="w1_i", align_bytes=64, bufs=4)
             nc.vector.tensor_copy(
-                out=w1_i[g][:, h].rearrange("p t m j -> p m j t"),
-                in_=w1_raw[g][:, :, 512 * h : 512 * (h + 1)].rearrange("p j (m t) -> p m j t", t=4),
+                out=w1_i[g][:, h].rearrange("p t m j -> p m t j"),
+                in_=w1_raw[g][:, :, 512 * h : 512 * (h + 1)].rearrange("p j (m t) -> p m t j", t=4),
             )
 
         def w1_quantise(g, h):
@@ -266,7 +270,7 @@ def tile_hebbianlayer_pb_kernel(
             part = slice(P * (jb % 2), P * (jb % 2 + 1))
             if jb % 2 == 0:
                 if c == SER:
-                    ser_out = stage.tile([P, BB, 2 * P], F32, tag="wide", name="ser_out", bufs=4, align_bytes=64)
+                    ser_out = stage.tile([P, BB, 2 * P], F32, tag="wide", name="ser_out", bufs=5, align_bytes=64)
                     outs[c] = ser_out[:]
                 else:
                     outs[c] = pred[:, jb // 2, c].rearrange("p h b -> p (h b)").rearrange("p (bb j) -> p bb j", bb=BB)
@@ -275,7 +279,9 @@ def tile_hebbianlayer_pb_kernel(
                 nc.vector.tensor_tensor(out=dst, in0=bank[:], in1=adds[c][:, :, jcols], op=ALU.add)
             else:
                 nc.scalar.copy(out=dst, in_=bank[:])
-            if jb % 2 == 1:
+            if jb // 2 == JP - 1 and c != SER:
+                nc.sync.dma_start(out=out_v[c][:, :, jcols], in_=dst)
+            elif jb % 2 == 1:
                 nc.sync.dma_start(out=out_v[c][:, :, P * (jb - 1) : P * (jb + 1)], in_=outs[c])
 
         inv = {}
@@ -318,12 +324,10 @@ def tile_hebbianlayer_pb_kernel(
         W(1)
         I(0)
         W(2)
+        I(1)
         act_turn(0)
         act_turn(1)
-        nc.vector.tensor_copy(out=b1f[:], in_=b1_raw[:])
-        nc.vector.tensor_copy(out=b2f[:], in_=b2_raw[:])
         Q(0)
-        I(1)
         act_quantise(0)
         act_quantise(1)
         Q(1)
@@ -335,35 +339,37 @@ def tile_hebbianlayer_pb_kernel(
         w1_quantise(0, 1)
         w1_interleave(1, 1)
         w1_quantise(1, 0)
-        I(2)
+        nc.vector.tensor_copy(out=b1f[:], in_=b1_raw[:])
+        nc.vector.tensor_copy(out=b2f[:], in_=b2_raw[:])
         w1_quantise(1, 1)
+        I(2)
         W(4)
         W(5)
         I(3)
         Q(2)
         load_w2()
+        load_w2()
+        W(6)
         hidden(0)
         hidden(1)
         Q(3)
         I(4)
-        W(6)
-        Q(4)
         hidden_interleave(0)
-        I(5)
+        Q(4)
         hidden_quantise(0)
         hidden_interleave(1)
-        Q(5)
+        I(5)
         hidden_quantise(1)
-        load_w2()
         W(7)
+        Q(5)
         I(6)
+        load_w2()
         load_w2()
         load_add(SER, serotonin)
         load_add(DOP, dopamine)
         load_add(GLU, glutamate)
         load_add(GAB, gaba)
         order = [(jb, c) for jb in range(8) for c in (SER, DOP, GLU, GAB)]
-        done = 0
         for i in range(7, 16):
             if i + 1 < 16:
                 W(i + 1)
@@ -371,39 +377,35 @@ def tile_hebbianlayer_pb_kernel(
             Q(i - 1)
             for k in range(DUE[i - 7]):
                 predict(*order.pop(0))
-            for k in range(SERDUE[i - 7]):
-                turn(done, SER)
-                if done > 0:
-                    finish(done - 1, SER)
-                done += 1
+        for jb in range(4):
+            turn(jb, SER)
         Q(15)
-        while order[0][0] < 7:
-            predict(*order.pop(0))
-        while done < 7:
-            turn(done, SER)
-            finish(done - 1, SER)
-            done += 1
-        predict(*order.pop(0))
-        turn(7, SER)
         while order:
             predict(*order.pop(0))
-        finish(6, SER)
-        finish(7, SER)
+        finish(0, SER)
+        finish(1, SER)
+        turn(4, SER)
+        turn(5, SER)
+        finish(2, SER)
+        finish(3, SER)
+        turn(6, SER)
+        turn(7, SER)
+        for jb in range(4, 8):
+            finish(jb, SER)
         invert(0)
-        square(0)
+        square(0, True)
         invert(1)
         square(1)
-        for jp in range(4):
-            for c in (DOP, GLU, GAB):
-                scale(jp, c)
-                if c == DOP and jp + 2 < 4:
-                    invert(jp + 2)
-                    square(jp + 2)
-                for jb in (2 * jp, 2 * jp + 1):
-                    turn(jb, c, "mm" if c == GLU else "tr")
-                if c == GLU:
-                    for jb in (2 * jp, 2 * jp + 1):
-                        finish(jb, DOP)
-            for c in (GLU, GAB):
-                for jb in (2 * jp, 2 * jp + 1):
-                    finish(jb, c)
+        tiles = [(jp, c) for jp in range(4) for c in (DOP, GLU, GAB)]
+        for k, (jp, c) in enumerate(tiles):
+            scale(jp, c)
+            if c == DOP and jp + 2 < 4:
+                invert(jp + 2)
+                square(jp + 2)
+            for jb in (2 * jp, 2 * jp + 1):
+                turn(jb, c, ("tr", "mm")[k % 2])
+            if k > 0:
+                for h in range(2):
+                    finish(2 * tiles[k - 1][0] + h, tiles[k - 1][1])
+        for h in range(2):
+            finish(6 + h, GAB)

@@ -24,9 +24,9 @@ DOP, SER, GLU, GAB = 0, 1, 2, 3
 FLOPS = 2 * B * D * D + 2 * B * D * NM * E
 
 JP = JB // 2
-WIDEN_ON_VECTOR = (4, 0, 0, 0, 0, 0, 0, 1, 1, 2, 2, 2, 2, 2, 2, 2)
+WIDEN_ON_VECTOR = (4, 0, 0, 0, 0, 0, 0, 1, 1, 1, 1, 1, 2, 2, 2, 2)
 DUE = (2, 2, 3, 3, 3, 3, 4, 4, 4)
-EVAC_ON_VECTOR = tuple((jb, SER) for jb in range(8)) + tuple((jb, GAB) for jb in (0, 2, 4, 6)) + ((6, GLU),)
+SER_ON_SCALAR = (0, 1, 2, 3, 4, 7)
 
 
 def tile_hebbianlayer_pb_kernel(
@@ -109,24 +109,24 @@ def tile_hebbianlayer_pb_kernel(
         wide = {}
         inter = {}
 
-        def widen(jb, g, nv):
-            t = stage.tile([P, 4, 4 * P], BF16, tag="wide", name="w2_wide", align_bytes=64, bufs=5)
-            wide[jb, g] = t
+        def widen(jb, g, j, engine):
+            if (jb, g) not in wide:
+                wide[jb, g] = stage.tile([P, 4, 4 * P], BF16, tag="wide", name="w2_wide", align_bytes=64, bufs=5)
+            t = wide[jb, g]
             half = 512 * (jb % 2)
-            for j in range(4):
-                src = w2b[2 * (jb // 2) + g][:, j, half : half + 512].bitcast(FP8)
-                if j < nv:
-                    nc.vector.tensor_scalar(
-                        out=t[:, j, :], in0=src, scalar1=w2s[:, g, j : j + 1], scalar2=None, op0=ALU.mult
-                    )
-                else:
-                    nc.scalar.activation(out=t[:, j, :], in_=src, func=ACT.Copy, scale=w2s[:, g, j : j + 1])
+            src = w2b[2 * (jb // 2) + g][:, j, half : half + 512].bitcast(FP8)
+            if engine == "V":
+                nc.vector.tensor_scalar(
+                    out=t[:, j, :], in0=src, scalar1=w2s[:, g, j : j + 1], scalar2=None, op0=ALU.mult
+                )
+            else:
+                nc.scalar.activation(out=t[:, j, :], in_=src, func=ACT.Copy, scale=w2s[:, g, j : j + 1])
 
         def interleave(jb, g):
             inter[jb, g] = stage.tile([P, NM, P, 4], BF16, tag="inter", name="w2_i", align_bytes=64, bufs=3)
             nc.vector.tensor_copy(
-                out=inter[jb, g][:].rearrange("p c m t -> p m c t"),
-                in_=wide[jb, g][:].rearrange("p t (m c) -> p m c t", c=NM),
+                out=inter[jb, g][:].rearrange("p c m t -> p m t c"),
+                in_=wide[jb, g][:].rearrange("p t (m c) -> p m t c", c=NM),
             )
 
         def quantise(jb, g):
@@ -141,20 +141,19 @@ def tile_hebbianlayer_pb_kernel(
         act_i = stage.tile([P, G, B, 4], BF16, tag="big", name="act_i", align_bytes=64, bufs=4)
         act_iw = act_i[:].rearrange("p g b t -> p g (b t)").bitcast(F32)
 
-        def act_turn(h):
-            for g in range(G):
-                bank = psum.tile([P, 2, 2, P], F32, tag="tr", name="act_t")
-                for i in range(2):
-                    for u in range(2):
-                        nc.tensor.transpose(
-                            bank[:, i, u, :], words[:, 2 * h + i, 256 * g + u : 256 * (g + 1) : 2], ident[:]
-                        )
-                dst = act_iw[:, g, 512 * h : 512 * (h + 1)].rearrange("p (i r u) -> p i r u", i=2, u=2)
-                src = bank[:].rearrange("p i u r -> p i r u")
-                if g == 0:
-                    nc.scalar.copy(out=dst, in_=src)
-                else:
-                    nc.vector.tensor_copy(out=dst, in_=src)
+        def act_turn(h, g, engine):
+            bank = psum.tile([P, 2, 2, P], F32, tag="tr", name="act_t")
+            for i in range(2):
+                for u in range(2):
+                    nc.tensor.transpose(
+                        bank[:, i, u, :], words[:, 2 * h + i, 256 * g + u : 256 * (g + 1) : 2], ident[:]
+                    )
+            dst = act_iw[:, g, 512 * h : 512 * (h + 1)].rearrange("p (i r u) -> p i r u", i=2, u=2)
+            src = bank[:].rearrange("p i u r -> p i r u")
+            if engine == "S":
+                nc.scalar.copy(out=dst, in_=src)
+            else:
+                nc.vector.tensor_copy(out=dst, in_=src)
 
         def act_quantise(g):
             nc.vector.quantize_mx(
@@ -166,11 +165,11 @@ def tile_hebbianlayer_pb_kernel(
         w1_i = {}
 
         def w1_interleave(g, h):
-            if h == 0:
+            if g not in w1_i:
                 w1_i[g] = stage.tile([P, 2, 4, P, 4], BF16, tag="big", name="w1_i", align_bytes=64, bufs=4)
             nc.vector.tensor_copy(
-                out=w1_i[g][:, h].rearrange("p t m j -> p m t j"),
-                in_=w1_raw[g][:, :, 512 * h : 512 * (h + 1)].rearrange("p j (m t) -> p m t j", t=4),
+                out=w1_i[g][:, h].rearrange("p t m j -> p m j t"),
+                in_=w1_raw[g][:, :, 512 * h : 512 * (h + 1)].rearrange("p j (m t) -> p m j t", t=4),
             )
 
         def w1_quantise(g, h):
@@ -183,31 +182,35 @@ def tile_hebbianlayer_pb_kernel(
 
         hid = {}
 
-        def hidden(h, on_vector=()):
-            if h == 0:
+        def hidden(h, t, engine):
+            if 0 not in hid:
                 hid[0] = stage.tile([P, G, 4, B], BF16, tag="big", name="hid", align_bytes=64, bufs=4)
-            for t in range(4):
-                bank = psum.tile([P, B], F32, tag="mm", name="mm")
-                cols = slice(512 * h + P * t, 512 * h + P * (t + 1))
-                for g in range(G):
-                    nc.tensor.matmul_mx(
-                        out=bank[:],
-                        lhsT=w1_c[:, g, cols].bitcast(FP8X4),
-                        lhsT_scale=w1_s[:, g, cols],
-                        rhs=act_c[:, g, :].bitcast(FP8X4),
-                        rhs_scale=act_s[:, g, :],
-                        start=(g == 0),
-                        stop=(g == G - 1),
-                    )
-                if t in on_vector:
-                    nc.vector.tensor_scalar(
-                        out=hid[0][:, h, t, :], in0=bank[:], scalar1=b1f[:, h, t : t + 1], scalar2=0.0, op0=ALU.add, op1=ALU.max
-                    )
-                else:
-                    nc.scalar.activation(out=hid[0][:, h, t, :], in_=bank[:], func=ACT.Relu, bias=b1f[:, h, t : t + 1])
+            bank = psum.tile([P, B], F32, tag="mm", name="mm")
+            cols = slice(512 * h + P * t, 512 * h + P * (t + 1))
+            for g in range(G):
+                nc.tensor.matmul_mx(
+                    out=bank[:],
+                    lhsT=w1_c[:, g, cols].bitcast(FP8X4),
+                    lhsT_scale=w1_s[:, g, cols],
+                    rhs=act_c[:, g, :].bitcast(FP8X4),
+                    rhs_scale=act_s[:, g, :],
+                    start=(g == 0),
+                    stop=(g == G - 1),
+                )
+            if engine == "V":
+                nc.vector.tensor_scalar(
+                    out=hid[0][:, h, t, :],
+                    in0=bank[:],
+                    scalar1=b1f[:, h, t : t + 1],
+                    scalar2=0.0,
+                    op0=ALU.add,
+                    op1=ALU.max,
+                )
+            else:
+                nc.scalar.activation(out=hid[0][:, h, t, :], in_=bank[:], func=ACT.Relu, bias=b1f[:, h, t : t + 1])
 
         def hidden_interleave(h):
-            if h == 0:
+            if 1 not in hid:
                 hid[1] = stage.tile([P, G, B, 4], BF16, tag="big", name="hid_i", align_bytes=64, bufs=4)
             nc.vector.tensor_copy(
                 out=hid[1][:, h].rearrange("p (n i) t -> p n t i", i=4),
@@ -241,6 +244,7 @@ def tile_hebbianlayer_pb_kernel(
             )
 
         outs = {}
+        stored = {}
         out_v = out.rearrange("(c bb p) j -> c p bb j", c=NM, bb=BB)
         banks = {}
 
@@ -251,7 +255,7 @@ def tile_hebbianlayer_pb_kernel(
                 bank = psum.tile([P, BB, P], F32, tag="mm", name="tr")
             banks[jb, c] = bank
             jcols = slice(P * jb, P * (jb + 1))
-            on_vector = (jb, c) in EVAC_ON_VECTOR
+            on_vector = c == SER and jb not in SER_ON_SCALAR
             if not on_vector:
                 nc.tensor.matmul(bank[:], lhsT=ident_bf[:], rhs=adds[c][:, :, jcols], start=True, stop=False)
             for bb in range(BB):
@@ -264,148 +268,317 @@ def tile_hebbianlayer_pb_kernel(
                     is_transpose=True,
                 )
 
-        def finish(jb, c):
+        def finish(jb, c, engine):
             bank = banks.pop((jb, c))
             jcols = slice(P * jb, P * (jb + 1))
             part = slice(P * (jb % 2), P * (jb % 2 + 1))
-            if jb % 2 == 0:
+            if (jb // 2, c) not in outs:
                 if c == SER:
                     ser_out = stage.tile([P, BB, 2 * P], F32, tag="wide", name="ser_out", bufs=5, align_bytes=64)
-                    outs[c] = ser_out[:]
+                    outs[jb // 2, c] = ser_out[:]
                 else:
-                    outs[c] = pred[:, jb // 2, c].rearrange("p h b -> p (h b)").rearrange("p (bb j) -> p bb j", bb=BB)
-            dst = outs[c][:, :, part]
-            if (jb, c) in EVAC_ON_VECTOR:
+                    outs[jb // 2, c] = pred[:, jb // 2, c].rearrange("p h b -> p (h b)").rearrange("p (bb j) -> p bb j", bb=BB)
+            dst = outs[jb // 2, c][:, :, part]
+            stored[jb // 2, c] = stored.get((jb // 2, c), 0) + 1
+            if c == SER and jb not in SER_ON_SCALAR:
                 nc.vector.tensor_tensor(out=dst, in0=bank[:], in1=adds[c][:, :, jcols], op=ALU.add)
+            elif engine == "V":
+                nc.vector.tensor_copy(out=dst, in_=bank[:])
             else:
                 nc.scalar.copy(out=dst, in_=bank[:])
             if jb // 2 == JP - 1 and c != SER:
                 nc.sync.dma_start(out=out_v[c][:, :, jcols], in_=dst)
-            elif jb % 2 == 1:
-                nc.sync.dma_start(out=out_v[c][:, :, P * (jb - 1) : P * (jb + 1)], in_=outs[c])
+            elif stored[jb // 2, c] == 2:
+                jb0 = jb - jb % 2
+                nc.sync.dma_start(out=out_v[c][:, :, P * jb0 : P * (jb0 + 2)], in_=outs[jb // 2, c])
 
         inv = {}
 
-        def invert(jp):
-            if jp % 2 == 0:
-                inv[jp // 2] = stage.tile([P, 2, 2, B], F32, tag="big", name="inv", align_bytes=64, bufs=4)
-            y = inv[jp // 2][:, jp % 2]
-            nc.scalar.activation(out=y, in_=pred[:, jp, SER], func=ACT.Abs_reciprocal_sqrt)
+        def invert(jb):
+            if jb // 4 not in inv:
+                inv[jb // 4] = stage.tile([P, 4, B], F32, tag="big", name="inv", align_bytes=64, bufs=4)
+            nc.scalar.activation(
+                out=inv[jb // 4][:, jb % 4, :], in_=pred[:, jb // 2, SER, jb % 2, :], func=ACT.Abs_reciprocal_sqrt
+            )
 
-        def square(jp, on_vector=False):
-            y = inv[jp // 2][:, jp % 2]
-            if on_vector:
+        def square(jb, engine):
+            y = inv[jb // 4][:, jb % 4, :]
+            if engine == "V":
                 nc.vector.tensor_tensor(out=y, in0=y, in1=y, op=ALU.mult)
             else:
                 nc.scalar.activation(out=y, in_=y, func=ACT.Square)
 
-        def scale(jp, c):
+        def scale(jb, c):
+            p_c = pred[:, jb // 2, c, jb % 2, :]
             nc.vector.scalar_tensor_tensor(
-                out=pred[:, jp, c],
-                in0=inv[jp // 2][:, jp % 2],
-                scalar=1e6,
-                in1=pred[:, jp, c],
-                op0=ALU.min,
-                op1=ALU.mult,
+                out=p_c, in0=inv[jb // 4][:, jb % 4, :], scalar=1e6, in1=p_c, op0=ALU.min, op1=ALU.mult
             )
 
-        units = [(0, 0), (1, 0), (0, 1), (1, 1)] + [(jb, g) for jb in range(2, 8) for g in range(2)]
-
-        def W(i):
-            widen(units[i][0], units[i][1], WIDEN_ON_VECTOR[i])
-
-        def I(i):
-            interleave(*units[i])
-
-        def Q(i):
-            quantise(*units[i])
-
-        W(0)
-        W(1)
-        I(0)
-        W(2)
-        I(1)
-        act_turn(0)
-        act_turn(1)
-        Q(0)
-        act_quantise(0)
-        act_quantise(1)
-        Q(1)
-        W(3)
+        widen(0, 0, 0, "S")
+        widen(0, 0, 1, "V")
+        widen(0, 0, 2, "S")
+        widen(0, 0, 3, "V")
+        widen(1, 0, 0, "V")
+        widen(1, 0, 1, "S")
+        widen(1, 0, 2, "S")
+        widen(1, 0, 3, "S")
+        load_w2()
+        widen(0, 1, 0, "S")
+        interleave(0, 0)
+        widen(0, 1, 1, "S")
+        widen(0, 1, 2, "S")
+        widen(0, 1, 3, "V")
+        act_turn(0, 0, "S")
+        interleave(1, 0)
+        act_turn(0, 1, "S")
+        interleave(0, 1)
+        act_turn(1, 0, "S")
         w1_interleave(0, 0)
         w1_interleave(0, 1)
+        widen(1, 1, 0, "S")
+        widen(1, 1, 1, "S")
+        act_turn(1, 1, "S")
+        widen(1, 1, 2, "S")
+        widen(1, 1, 3, "S")
+        load_w2()
+        widen(2, 0, 0, "S")
         w1_quantise(0, 0)
+        widen(2, 0, 1, "S")
         w1_interleave(1, 0)
+        widen(2, 0, 2, "S")
         w1_quantise(0, 1)
-        w1_interleave(1, 1)
+        widen(2, 0, 3, "V")
+        widen(2, 1, 0, "S")
+        act_quantise(0)
+        widen(2, 1, 1, "S")
+        quantise(0, 0)
+        widen(2, 1, 2, "S")
         w1_quantise(1, 0)
+        act_quantise(1)
+        quantise(1, 0)
+        widen(2, 1, 3, "S")
+        widen(3, 0, 0, "S")
+        widen(3, 0, 1, "S")
+        widen(3, 0, 2, "V")
+        widen(3, 0, 3, "S")
+        load_w2()
+        widen(3, 1, 0, "S")
+        w1_interleave(1, 1)
         nc.vector.tensor_copy(out=b1f[:], in_=b1_raw[:])
         nc.vector.tensor_copy(out=b2f[:], in_=b2_raw[:])
+        hidden(0, 0, "S")
+        widen(3, 1, 1, "S")
+        hidden(0, 1, "S")
+        hidden(0, 2, "S")
+        widen(3, 1, 2, "V")
+        quantise(0, 1)
+        hidden(0, 3, "S")
         w1_quantise(1, 1)
-        I(2)
-        W(4)
-        W(5)
-        I(3)
-        Q(2)
-        load_w2()
-        load_w2()
-        W(6)
-        hidden(0)
-        hidden(1)
-        Q(3)
-        I(4)
+        interleave(1, 1)
+        hidden(1, 0, "S")
         hidden_interleave(0)
-        Q(4)
-        hidden_quantise(0)
+        interleave(2, 0)
+        hidden(1, 1, "S")
+        hidden(1, 2, "S")
+        hidden(1, 3, "S")
         hidden_interleave(1)
-        I(5)
+        hidden_quantise(0)
         hidden_quantise(1)
-        W(7)
-        Q(5)
-        I(6)
-        load_w2()
+        widen(3, 1, 3, "S")
         load_w2()
         load_add(SER, serotonin)
         load_add(DOP, dopamine)
         load_add(GLU, glutamate)
         load_add(GAB, gaba)
-        order = [(jb, c) for jb in range(8) for c in (SER, DOP, GLU, GAB)]
-        for i in range(7, 16):
-            if i + 1 < 16:
-                W(i + 1)
-            I(i)
-            Q(i - 1)
-            for k in range(DUE[i - 7]):
-                predict(*order.pop(0))
-        for jb in range(4):
-            turn(jb, SER)
-        Q(15)
-        while order:
-            predict(*order.pop(0))
-        finish(0, SER)
-        finish(1, SER)
-        turn(4, SER)
-        turn(5, SER)
-        finish(2, SER)
-        finish(3, SER)
-        turn(6, SER)
-        turn(7, SER)
-        for jb in range(4, 8):
-            finish(jb, SER)
+        widen(4, 0, 0, "S")
+        widen(4, 0, 1, "S")
+        widen(4, 0, 2, "S")
+        interleave(2, 1)
+        widen(4, 0, 3, "S")
+        quantise(1, 1)
+        quantise(2, 0)
+        widen(4, 1, 0, "S")
+        widen(4, 1, 1, "S")
+        widen(4, 1, 2, "V")
+        interleave(3, 0)
+        widen(4, 1, 3, "S")
+        widen(5, 0, 0, "S")
+        quantise(2, 1)
+        interleave(3, 1)
+        predict(0, SER)
+        quantise(3, 0)
+        widen(5, 0, 1, "S")
+        widen(5, 0, 2, "S")
+        widen(5, 0, 3, "V")
+        interleave(4, 0)
+        predict(0, DOP)
+        interleave(4, 1)
+        widen(5, 1, 0, "V")
+        quantise(3, 1)
+        predict(0, GLU)
+        predict(0, GAB)
+        predict(1, SER)
+        widen(5, 1, 1, "V")
+        predict(1, DOP)
+        quantise(4, 0)
+        turn(0, SER, "tr")
+        predict(1, GLU)
+        predict(1, GAB)
+        predict(2, SER)
+        widen(5, 1, 2, "V")
+        widen(5, 1, 3, "S")
+        predict(2, DOP)
+        turn(1, SER, "tr")
+        predict(2, GLU)
+        finish(0, SER, "S")
+        quantise(4, 1)
+        interleave(5, 0)
+        widen(6, 0, 0, "V")
+        predict(2, GAB)
+        finish(1, SER, "S")
+        widen(6, 0, 1, "V")
+        predict(3, SER)
+        widen(6, 0, 2, "V")
+        widen(6, 0, 3, "V")
+        turn(2, SER, "tr")
+        predict(3, DOP)
+        widen(6, 1, 0, "V")
+        predict(3, GLU)
+        widen(6, 1, 1, "V")
+        predict(3, GAB)
+        interleave(5, 1)
+        widen(6, 1, 2, "V")
+        widen(6, 1, 3, "V")
+        predict(4, SER)
         invert(0)
-        square(0, True)
         invert(1)
-        square(1)
-        tiles = [(jp, c) for jp in range(4) for c in (DOP, GLU, GAB)]
-        for k, (jp, c) in enumerate(tiles):
-            scale(jp, c)
-            if c == DOP and jp + 2 < 4:
-                invert(jp + 2)
-                square(jp + 2)
-            for jb in (2 * jp, 2 * jp + 1):
-                turn(jb, c, ("tr", "mm")[k % 2])
-            if k > 0:
-                for h in range(2):
-                    finish(2 * tiles[k - 1][0] + h, tiles[k - 1][1])
-        for h in range(2):
-            finish(6 + h, GAB)
+        interleave(6, 0)
+        square(0, "S")
+        turn(3, SER, "tr")
+        quantise(5, 0)
+        invert(2)
+        widen(7, 0, 0, "V")
+        invert(3)
+        invert(4)
+        square(1, "S")
+        predict(4, DOP)
+        widen(7, 0, 1, "V")
+        square(2, "S")
+        scale(0, DOP)
+        widen(7, 0, 2, "V")
+        widen(7, 0, 3, "V")
+        predict(4, GLU)
+        widen(7, 1, 0, "V")
+        turn(0, DOP, "tr")
+        predict(4, GAB)
+        finish(2, SER, "S")
+        widen(7, 1, 1, "V")
+        quantise(5, 1)
+        scale(1, DOP)
+        scale(0, GLU)
+        predict(5, SER)
+        scale(1, GLU)
+        turn(1, DOP, "tr")
+        interleave(6, 1)
+        widen(7, 1, 2, "V")
+        finish(3, SER, "S")
+        predict(5, DOP)
+        quantise(6, 0)
+        quantise(6, 1)
+        widen(7, 1, 3, "V")
+        predict(5, GLU)
+        turn(4, SER, "mm")
+        finish(4, SER, "S")
+        finish(0, DOP, "S")
+        predict(5, GAB)
+        turn(0, GLU, "tr")
+        interleave(7, 0)
+        scale(0, GAB)
+        scale(1, GAB)
+        turn(5, SER, "mm")
+        interleave(7, 1)
+        turn(1, GLU, "tr")
+        finish(5, SER, "V")
+        predict(6, SER)
+        finish(1, DOP, "S")
+        turn(0, GAB, "tr")
+        finish(0, GLU, "S")
+        predict(6, DOP)
+        predict(6, GLU)
+        turn(6, SER, "tr")
+        quantise(7, 0)
+        quantise(7, 1)
+        turn(1, GAB, "tr")
+        square(3, "S")
+        finish(1, GLU, "S")
+        scale(2, DOP)
+        finish(6, SER, "V")
+        finish(0, GAB, "V")
+        predict(6, GAB)
+        predict(7, SER)
+        predict(7, DOP)
+        predict(7, GLU)
+        predict(7, GAB)
+        scale(3, DOP)
+        turn(2, DOP, "mm")
+        turn(3, DOP, "tr")
+        invert(5)
+        scale(2, GLU)
+        turn(7, SER, "mm")
+        finish(1, GAB, "V")
+        turn(2, GLU, "tr")
+        scale(3, GLU)
+        finish(2, DOP, "V")
+        finish(3, DOP, "V")
+        turn(3, GLU, "tr")
+        square(4, "V")
+        finish(7, SER, "S")
+        scale(2, GAB)
+        finish(2, GLU, "S")
+        turn(2, GAB, "tr")
+        scale(3, GAB)
+        turn(3, GAB, "mm")
+        square(5, "V")
+        scale(4, DOP)
+        finish(3, GLU, "S")
+        finish(2, GAB, "S")
+        turn(4, DOP, "mm")
+        scale(5, DOP)
+        scale(4, GLU)
+        scale(5, GLU)
+        invert(6)
+        finish(3, GAB, "S")
+        turn(5, DOP, "tr")
+        finish(4, DOP, "S")
+        turn(4, GLU, "tr")
+        scale(4, GAB)
+        square(6, "V")
+        turn(5, GLU, "tr")
+        scale(5, GAB)
+        turn(4, GAB, "mm")
+        finish(5, DOP, "S")
+        finish(4, GLU, "V")
+        turn(5, GAB, "mm")
+        invert(7)
+        finish(5, GLU, "S")
+        scale(6, DOP)
+        turn(6, DOP, "tr")
+        square(7, "S")
+        scale(7, DOP)
+        finish(4, GAB, "S")
+        scale(6, GLU)
+        scale(7, GLU)
+        turn(7, DOP, "mm")
+        turn(6, GLU, "mm")
+        turn(7, GLU, "tr")
+        scale(6, GAB)
+        finish(5, GAB, "S")
+        finish(6, DOP, "S")
+        finish(7, DOP, "S")
+        scale(7, GAB)
+        turn(6, GAB, "tr")
+        finish(6, GLU, "S")
+        turn(7, GAB, "tr")
+        finish(7, GLU, "V")
+        finish(6, GAB, "V")
+        finish(7, GAB, "S")

from contextlib import ExitStack

import concourse.mybir as mybir
from concourse.masks import make_identity

F32 = mybir.dt.float32
BF16 = mybir.dt.bfloat16
U32 = mybir.dt.uint32
U8 = mybir.dt.uint8
FP8 = mybir.dt.float8_e4m3fn
FP8X4 = mybir.dt.float8_e4m3fn_x4
ACT = mybir.ActivationFunctionType
ALU = mybir.AluOpType

P = 128
B, D, E, NM = 512, 1024, 1024, 4
G = 2
BB = 4
JB = 8
CW = 1024
HC = 8
DOP, SER, GLU, GAB = 0, 1, 2, 3

FLOPS = 2 * B * D * D + 2 * B * D * NM * E

JP = JB // 2
WIDEN_ON_VECTOR = (4, 0, 0, 0, 0, 0, 0, 1, 1, 1, 1, 1, 2, 2, 2, 2)
DUE = (2, 2, 3, 3, 3, 3, 4, 4, 4)
SER_ON_SCALAR = (0, 1, 2, 3, 4, 7)


def tile_hebbianlayer_pb_kernel(
    tc, prev_act, W1, b1, W2_bytes, W2_scale, b2, dopamine, serotonin, glutamate, gaba, out
):
    nc = tc.nc
    with ExitStack() as ctx:
        keep = ctx.enter_context(tc.tile_pool(name="keep", bufs=1))
        stage = ctx.enter_context(tc.tile_pool(name="stage", bufs=3))
        psum = ctx.enter_context(tc.psum_pool(name="psum", bufs=4))
        ctx.enter_context(tc.manual_schedule())

        ident = keep.tile([P, P], F32, name="ident")
        make_identity(nc, ident[:])
        ident_bf = keep.tile([P, P], BF16, name="ident_bf")
        nc.vector.tensor_copy(out=ident_bf[:], in_=ident[:])

        w2s = keep.tile([P, G, 4], F32, name="w2s")
        nc.scalar.dma_start(out=w2s[:], in_=W2_scale.rearrange("(g p t) o -> p g (t o)", g=G, p=P, t=4))
        b1_raw = keep.tile([P, G, 4], BF16, name="b1_raw")
        b2_raw = keep.tile([P, JB, NM], BF16, name="b2_raw")

        warm = keep.tile([P, 1], F32, name="warm")
        nc.vector.memset(warm[:], 0.0)
        nc.scalar.activation(out=warm[:], in_=warm[:], func=ACT.Tanh)

        w2_v = W2_bytes.rearrange("(g p t) n -> g p t n", g=G, p=P, t=4)
        w1_v = W1.rearrange("(g p t) n -> g p t n", g=G, p=P, t=4)
        act_v = prev_act.rearrange("(bb p) k -> p bb k", p=P)
        w2b = []

        def load_w2():
            hc = len(w2b)
            ch, g = divmod(hc, 2)
            t = stage.tile([P, 4, CW], U8, tag="w2bytes", name="w2bytes", bufs=4)
            if hc == 0:
                for h in range(2):
                    cols = slice(512 * h, 512 * (h + 1))
                    nc.sync.dma_start(out=t[:, :, cols], in_=w2_v[g][:, :, cols])
            else:
                nc.sync.dma_start(out=t[:], in_=w2_v[g][:, :, ch * CW : (ch + 1) * CW])
            w2b.append(t)

        load_w2()
        load_w2()
        act_raw = stage.tile([P, BB, D], BF16, tag="big", name="act_raw", align_bytes=64, bufs=4)
        for h in range(2):
            nc.sync.dma_start(out=act_raw[:, 2 * h : 2 * h + 2, :], in_=act_v[:, 2 * h : 2 * h + 2, :])
        w1_raw = []

        def load_w1(g):
            t = stage.tile([P, 4, D], BF16, tag="big", name="w1_raw", align_bytes=64, bufs=4)
            nc.sync.dma_start(out=t[:], in_=w1_v[g])
            w1_raw.append(t)

        load_w1(0)
        load_w1(1)
        nc.sync.dma_start(out=b1_raw[:], in_=b1.rearrange("(g p t) -> p g t", g=G, p=P, t=4))
        nc.sync.dma_start(out=b2_raw[:], in_=b2.rearrange("(jb p c) -> p jb c", jb=JB, p=P, c=NM))
        for i in range(2):
            load_w2()
        adds = {}

        def load_add(c, src):
            adds[c] = keep.tile([P, BB, E], BF16, name="add_%d" % c)
            nc.sync.dma_start(out=adds[c][:], in_=src.rearrange("(bb p) j -> p bb j", p=P))

        act_c = keep.tile([P, G, B], U32, name="act_c", align_bytes=64)
        act_s = keep.tile([P, G, B], U8, name="act_s", align_bytes=64)
        w1_c = keep.tile([P, G, D], U32, name="w1_c", align_bytes=64)
        w1_s = keep.tile([P, G, D], U8, name="w1_s", align_bytes=64)
        hid_c = keep.tile([P, G, B], U32, name="hid_c", align_bytes=64)
        hid_s = keep.tile([P, G, B], U8, name="hid_s", align_bytes=64)
        w2_c = keep.tile([P, G, NM * E], U32, name="w2_c", align_bytes=64)
        w2_s = keep.tile([P, G, NM * E], U8, name="w2_s", align_bytes=64)

        b1f = keep.tile([P, G, 4], F32, name="b1f")
        b2f = keep.tile([P, JB, NM], F32, name="b2f")

        wide = {}
        inter = {}

        def widen(jb, g, j, engine):
            if (jb, g) not in wide:
                wide[jb, g] = stage.tile([P, 4, 4 * P], BF16, tag="wide", name="w2_wide", align_bytes=64, bufs=5)
            t = wide[jb, g]
            half = 512 * (jb % 2)
            src = w2b[2 * (jb // 2) + g][:, j, half : half + 512].bitcast(FP8)
            if engine == "V":
                nc.vector.tensor_scalar(
                    out=t[:, j, :], in0=src, scalar1=w2s[:, g, j : j + 1], scalar2=None, op0=ALU.mult
                )
            else:
                nc.scalar.activation(out=t[:, j, :], in_=src, func=ACT.Copy, scale=w2s[:, g, j : j + 1])

        def interleave(jb, g):
            inter[jb, g] = stage.tile([P, NM, P, 4], BF16, tag="inter", name="w2_i", align_bytes=64, bufs=3)
            nc.vector.tensor_copy(
                out=inter[jb, g][:].rearrange("p c m t -> p m t c"),
                in_=wide[jb, g][:].rearrange("p t (m c) -> p m t c", c=NM),
            )

        def quantise(jb, g):
            cols = slice(512 * jb, 512 * (jb + 1))
            nc.vector.quantize_mx(
                out=w2_c[:, g, cols].bitcast(FP8X4),
                scales=w2_s[:, g, cols],
                in_=inter[jb, g][:].rearrange("p c m t -> p (c m t)"),
            )

        words = act_raw[:].bitcast(F32)
        act_i = stage.tile([P, G, B, 4], BF16, tag="big", name="act_i", align_bytes=64, bufs=4)
        act_iw = act_i[:].rearrange("p g b t -> p g (b t)").bitcast(F32)

        def act_turn(h, g, engine):
            bank = psum.tile([P, 2, 2, P], F32, tag="tr", name="act_t")
            for i in range(2):
                for u in range(2):
                    nc.tensor.transpose(
                        bank[:, i, u, :], words[:, 2 * h + i, 256 * g + u : 256 * (g + 1) : 2], ident[:]
                    )
            dst = act_iw[:, g, 512 * h : 512 * (h + 1)].rearrange("p (i r u) -> p i r u", i=2, u=2)
            src = bank[:].rearrange("p i u r -> p i r u")
            if engine == "S":
                nc.scalar.copy(out=dst, in_=src)
            else:
                nc.vector.tensor_copy(out=dst, in_=src)

        def act_quantise(g):
            nc.vector.quantize_mx(
                out=act_c[:, g, :].bitcast(FP8X4),
                scales=act_s[:, g, :],
                in_=act_i[:, g].rearrange("p b t -> p (b t)"),
            )

        w1_i = {}

        def w1_interleave(g, h):
            if g not in w1_i:
                w1_i[g] = stage.tile([P, 2, 4, P, 4], BF16, tag="big", name="w1_i", align_bytes=64, bufs=4)
            nc.vector.tensor_copy(
                out=w1_i[g][:, h].rearrange("p t m j -> p m j t"),
                in_=w1_raw[g][:, :, 512 * h : 512 * (h + 1)].rearrange("p j (m t) -> p m j t", t=4),
            )

        def w1_quantise(g, h):
            cols = slice(512 * h, 512 * (h + 1))
            nc.vector.quantize_mx(
                out=w1_c[:, g, cols].bitcast(FP8X4),
                scales=w1_s[:, g, cols],
                in_=w1_i[g][:, h].rearrange("p t m j -> p (t m j)"),
            )

        hid = {}

        def hidden(h, t, engine):
            if 0 not in hid:
                hid[0] = stage.tile([P, G, 4, B], BF16, tag="big", name="hid", align_bytes=64, bufs=4)
            bank = psum.tile([P, B], F32, tag="mm", name="mm")
            cols = slice(512 * h + P * t, 512 * h + P * (t + 1))
            for g in range(G):
                nc.tensor.matmul_mx(
                    out=bank[:],
                    lhsT=w1_c[:, g, cols].bitcast(FP8X4),
                    lhsT_scale=w1_s[:, g, cols],
                    rhs=act_c[:, g, :].bitcast(FP8X4),
                    rhs_scale=act_s[:, g, :],
                    start=(g == 0),
                    stop=(g == G - 1),
                )
            if engine == "V":
                nc.vector.tensor_scalar(
                    out=hid[0][:, h, t, :],
                    in0=bank[:],
                    scalar1=b1f[:, h, t : t + 1],
                    scalar2=0.0,
                    op0=ALU.add,
                    op1=ALU.max,
                )
            else:
                nc.scalar.activation(out=hid[0][:, h, t, :], in_=bank[:], func=ACT.Relu, bias=b1f[:, h, t : t + 1])

        def hidden_interleave(h):
            if 1 not in hid:
                hid[1] = stage.tile([P, G, B, 4], BF16, tag="big", name="hid_i", align_bytes=64, bufs=4)
            nc.vector.tensor_copy(
                out=hid[1][:, h].rearrange("p (n i) t -> p n t i", i=4),
                in_=hid[0][:, h].rearrange("p t (n i) -> p n t i", i=4),
            )

        def hidden_quantise(h):
            nc.vector.quantize_mx(
                out=hid_c[:, h, :].bitcast(FP8X4),
                scales=hid_s[:, h, :],
                in_=hid[1][:, h].rearrange("p b t -> p (b t)"),
            )

        pred = keep.tile([P, JP, NM, 2, B], F32, name="pred")

        def predict(jb, c):
            bank = psum.tile([P, B], F32, tag="mm", name="mm")
            cols = slice(512 * jb + P * c, 512 * jb + P * (c + 1))
            for g in range(G):
                nc.tensor.matmul_mx(
                    out=bank[:],
                    lhsT=w2_c[:, g, cols].bitcast(FP8X4),
                    lhsT_scale=w2_s[:, g, cols],
                    rhs=hid_c[:, g, :].bitcast(FP8X4),
                    rhs_scale=hid_s[:, g, :],
                    start=(g == 0),
                    stop=(g == G - 1),
                )
            nc.scalar.activation(
                out=pred[:, jb // 2, c, jb % 2, :], in_=bank[:], func=ACT.Tanh, bias=b2f[:, jb, c : c + 1]
            )

        outs = {}
        stored = {}
        out_v = out.rearrange("(c bb p) j -> c p bb j", c=NM, bb=BB)
        banks = {}

        def turn(jb, c, tag="tr"):
            if tag == "tr":
                bank = psum.tile([P, BB, P], F32, tag="tr", name="tr")
            else:
                bank = psum.tile([P, BB, P], F32, tag="mm", name="tr")
            banks[jb, c] = bank
            jcols = slice(P * jb, P * (jb + 1))
            on_vector = c == SER and jb not in SER_ON_SCALAR
            if not on_vector:
                nc.tensor.matmul(bank[:], lhsT=ident_bf[:], rhs=adds[c][:, :, jcols], start=True, stop=False)
            for bb in range(BB):
                nc.tensor.matmul(
                    bank[:, bb, :],
                    lhsT=pred[:, jb // 2, c, jb % 2, P * bb : P * (bb + 1)],
                    rhs=ident[:],
                    start=on_vector,
                    stop=on_vector or bb == BB - 1,
                    is_transpose=True,
                )

        def finish(jb, c, engine):
            bank = banks.pop((jb, c))
            jcols = slice(P * jb, P * (jb + 1))
            part = slice(P * (jb % 2), P * (jb % 2 + 1))
            if (jb // 2, c) not in outs:
                if c == SER:
                    ser_out = stage.tile([P, BB, 2 * P], F32, tag="wide", name="ser_out", bufs=5, align_bytes=64)
                    outs[jb // 2, c] = ser_out[:]
                else:
                    outs[jb // 2, c] = pred[:, jb // 2, c].rearrange("p h b -> p (h b)").rearrange("p (bb j) -> p bb j", bb=BB)
            dst = outs[jb // 2, c][:, :, part]
            stored[jb // 2, c] = stored.get((jb // 2, c), 0) + 1
            if c == SER and jb not in SER_ON_SCALAR:
                nc.vector.tensor_tensor(out=dst, in0=bank[:], in1=adds[c][:, :, jcols], op=ALU.add)
            elif engine == "V":
                nc.vector.tensor_copy(out=dst, in_=bank[:])
            else:
                nc.scalar.copy(out=dst, in_=bank[:])
            if jb // 2 == JP - 1 and c != SER:
                nc.sync.dma_start(out=out_v[c][:, :, jcols], in_=dst)
            elif stored[jb // 2, c] == 2:
                jb0 = jb - jb % 2
                nc.sync.dma_start(out=out_v[c][:, :, P * jb0 : P * (jb0 + 2)], in_=outs[jb // 2, c])

        inv = {}

        def invert(jb):
            if jb // 4 not in inv:
                inv[jb // 4] = stage.tile([P, 4, B], F32, tag="big", name="inv", align_bytes=64, bufs=4)
            nc.scalar.activation(
                out=inv[jb // 4][:, jb % 4, :], in_=pred[:, jb // 2, SER, jb % 2, :], func=ACT.Abs_reciprocal_sqrt
            )

        def square(jb, engine):
            y = inv[jb // 4][:, jb % 4, :]
            if engine == "V":
                nc.vector.tensor_tensor(out=y, in0=y, in1=y, op=ALU.mult)
            else:
                nc.scalar.activation(out=y, in_=y, func=ACT.Square)

        def scale(jb, c):
            p_c = pred[:, jb // 2, c, jb % 2, :]
            nc.vector.scalar_tensor_tensor(
                out=p_c, in0=inv[jb // 4][:, jb % 4, :], scalar=1e6, in1=p_c, op0=ALU.min, op1=ALU.mult
            )

        widen(0, 0, 0, "S")
        widen(0, 0, 1, "V")
        widen(0, 0, 2, "S")
        widen(0, 0, 3, "V")
        widen(1, 0, 0, "V")
        widen(1, 0, 1, "S")
        widen(1, 0, 2, "S")
        widen(1, 0, 3, "S")
        load_w2()
        widen(0, 1, 0, "S")
        interleave(0, 0)
        widen(0, 1, 1, "S")
        widen(0, 1, 2, "S")
        widen(0, 1, 3, "V")
        act_turn(0, 0, "S")
        interleave(1, 0)
        act_turn(0, 1, "S")
        interleave(0, 1)
        act_turn(1, 0, "S")
        w1_interleave(0, 0)
        w1_interleave(0, 1)
        widen(1, 1, 0, "S")
        widen(1, 1, 1, "S")
        act_turn(1, 1, "S")
        widen(1, 1, 2, "S")
        widen(1, 1, 3, "S")
        load_w2()
        widen(2, 0, 0, "S")
        w1_quantise(0, 0)
        widen(2, 0, 1, "S")
        w1_interleave(1, 0)
        widen(2, 0, 2, "S")
        w1_quantise(0, 1)
        widen(2, 0, 3, "V")
        widen(2, 1, 0, "S")
        act_quantise(0)
        widen(2, 1, 1, "S")
        quantise(0, 0)
        widen(2, 1, 2, "S")
        w1_quantise(1, 0)
        act_quantise(1)
        quantise(1, 0)
        widen(2, 1, 3, "S")
        widen(3, 0, 0, "S")
        widen(3, 0, 1, "S")
        widen(3, 0, 2, "V")
        widen(3, 0, 3, "S")
        load_w2()
        widen(3, 1, 0, "S")
        w1_interleave(1, 1)
        nc.vector.tensor_copy(out=b1f[:], in_=b1_raw[:])
        nc.vector.tensor_copy(out=b2f[:], in_=b2_raw[:])
        hidden(0, 0, "S")
        widen(3, 1, 1, "S")
        hidden(0, 1, "S")
        hidden(0, 2, "S")
        widen(3, 1, 2, "V")
        quantise(0, 1)
        hidden(0, 3, "S")
        w1_quantise(1, 1)
        interleave(1, 1)
        hidden(1, 0, "S")
        hidden_interleave(0)
        interleave(2, 0)
        hidden(1, 1, "S")
        hidden(1, 2, "S")
        hidden(1, 3, "S")
        hidden_interleave(1)
        hidden_quantise(0)
        hidden_quantise(1)
        widen(3, 1, 3, "S")
        load_w2()
        load_add(SER, serotonin)
        load_add(DOP, dopamine)
        load_add(GLU, glutamate)
        load_add(GAB, gaba)
        widen(4, 0, 0, "S")
        widen(4, 0, 1, "S")
        widen(4, 0, 2, "S")
        interleave(2, 1)
        widen(4, 0, 3, "S")
        quantise(1, 1)
        quantise(2, 0)
        widen(4, 1, 0, "S")
        widen(4, 1, 1, "S")
        widen(4, 1, 2, "V")
        interleave(3, 0)
        widen(4, 1, 3, "S")
        widen(5, 0, 0, "S")
        quantise(2, 1)
        interleave(3, 1)
        predict(0, SER)
        quantise(3, 0)
        widen(5, 0, 1, "S")
        widen(5, 0, 2, "S")
        widen(5, 0, 3, "V")
        interleave(4, 0)
        predict(0, DOP)
        interleave(4, 1)
        widen(5, 1, 0, "V")
        quantise(3, 1)
        predict(0, GLU)
        predict(0, GAB)
        predict(1, SER)
        widen(5, 1, 1, "V")
        predict(1, DOP)
        quantise(4, 0)
        turn(0, SER, "tr")
        predict(1, GLU)
        predict(1, GAB)
        predict(2, SER)
        widen(5, 1, 2, "V")
        widen(5, 1, 3, "S")
        predict(2, DOP)
        turn(1, SER, "tr")
        predict(2, GLU)
        finish(0, SER, "S")
        quantise(4, 1)
        interleave(5, 0)
        widen(6, 0, 0, "V")
        predict(2, GAB)
        finish(1, SER, "S")
        widen(6, 0, 1, "V")
        predict(3, SER)
        widen(6, 0, 2, "V")
        widen(6, 0, 3, "V")
        turn(2, SER, "tr")
        predict(3, DOP)
        widen(6, 1, 0, "V")
        predict(3, GLU)
        widen(6, 1, 1, "V")
        predict(3, GAB)
        interleave(5, 1)
        widen(6, 1, 2, "V")
        widen(6, 1, 3, "V")
        predict(4, SER)
        invert(0)
        invert(1)
        interleave(6, 0)
        square(0, "S")
        turn(3, SER, "tr")
        quantise(5, 0)
        invert(2)
        widen(7, 0, 0, "V")
        invert(3)
        invert(4)
        square(1, "S")
        predict(4, DOP)
        widen(7, 0, 1, "V")
        square(2, "S")
        scale(0, DOP)
        widen(7, 0, 2, "V")
        widen(7, 0, 3, "V")
        predict(4, GLU)
        widen(7, 1, 0, "V")
        turn(0, DOP, "tr")
        predict(4, GAB)
        finish(2, SER, "S")
        widen(7, 1, 1, "V")
        quantise(5, 1)
        scale(1, DOP)
        scale(0, GLU)
        predict(5, SER)
        scale(1, GLU)
        turn(1, DOP, "tr")
        interleave(6, 1)
        widen(7, 1, 2, "V")
        finish(3, SER, "S")
        predict(5, DOP)
        quantise(6, 0)
        quantise(6, 1)
        widen(7, 1, 3, "V")
        predict(5, GLU)
        turn(4, SER, "mm")
        finish(4, SER, "S")
        finish(0, DOP, "S")
        predict(5, GAB)
        turn(0, GLU, "tr")
        interleave(7, 0)
        scale(0, GAB)
        scale(1, GAB)
        turn(5, SER, "mm")
        interleave(7, 1)
        turn(1, GLU, "tr")
        finish(5, SER, "V")
        predict(6, SER)
        finish(1, DOP, "S")
        turn(0, GAB, "tr")
        finish(0, GLU, "S")
        predict(6, DOP)
        predict(6, GLU)
        turn(6, SER, "tr")
        quantise(7, 0)
        quantise(7, 1)
        turn(1, GAB, "tr")
        square(3, "S")
        finish(1, GLU, "S")
        scale(2, DOP)
        finish(6, SER, "V")
        finish(0, GAB, "V")
        predict(6, GAB)
        predict(7, SER)
        predict(7, DOP)
        predict(7, GLU)
        predict(7, GAB)
        scale(3, DOP)
        turn(2, DOP, "mm")
        turn(3, DOP, "tr")
        invert(5)
        scale(2, GLU)
        turn(7, SER, "mm")
        finish(1, GAB, "V")
        turn(2, GLU, "tr")
        scale(3, GLU)
        finish(2, DOP, "V")
        finish(3, DOP, "V")
        turn(3, GLU, "tr")
        square(4, "V")
        finish(7, SER, "S")
        scale(2, GAB)
        finish(2, GLU, "S")
        turn(2, GAB, "tr")
        scale(3, GAB)
        turn(3, GAB, "mm")
        square(5, "V")
        scale(4, DOP)
        finish(3, GLU, "S")
        finish(2, GAB, "S")
        turn(4, DOP, "mm")
        scale(5, DOP)
        scale(4, GLU)
        scale(5, GLU)
        invert(6)
        finish(3, GAB, "S")
        turn(5, DOP, "tr")
        finish(4, DOP, "S")
        turn(4, GLU, "tr")
        scale(4, GAB)
        square(6, "V")
        turn(5, GLU, "tr")
        scale(5, GAB)
        turn(4, GAB, "mm")
        finish(5, DOP, "S")
        finish(4, GLU, "V")
        turn(5, GAB, "mm")
        invert(7)
        finish(5, GLU, "S")
        scale(6, DOP)
        turn(6, DOP, "tr")
        square(7, "S")
        scale(7, DOP)
        finish(4, GAB, "S")
        scale(6, GLU)
        scale(7, GLU)
        turn(7, DOP, "mm")
        turn(6, GLU, "mm")
        turn(7, GLU, "tr")
        scale(6, GAB)
        finish(5, GAB, "S")
        finish(6, DOP, "S")
        finish(7, DOP, "S")
        scale(7, GAB)
        turn(6, GAB, "tr")
        finish(6, GLU, "S")
        turn(7, GAB, "tr")
        finish(7, GLU, "V")
        finish(6, GAB, "V")
        finish(7, GAB, "S")
